import numpy as np
import ml_dtypes


def mxq(x, axis, fmt="e4m3"):
    dtype, down = {"e4m3": (ml_dtypes.float8_e4m3fn, 7), "e5m2": (ml_dtypes.float8_e5m2, 14)}[fmt]
    v = np.moveaxis(np.asarray(x, np.float32).astype(ml_dtypes.bfloat16).astype(np.float64), axis, -1)
    blocks = v.reshape(v.shape[:-1] + (-1, 32))
    amax = np.abs(blocks).max(-1, keepdims=True)
    byte = np.maximum(np.where(amax > 0, np.frexp(amax)[1] - 1 + 127, 0) - down, 1)
    scale = np.exp2(byte - 127.0)
    codes = (blocks / scale).astype(np.float32).astype(dtype).astype(np.float64)
    return np.moveaxis((codes * scale).reshape(v.shape), -1, axis)


WIDE = False


def mx_kscale(k):
    if not WIDE:
        return np.ones(k)
    levels = np.array([30, -30])
    if k % 512:
        return np.exp2(np.random.permutation(np.resize(levels, k // 32))).repeat(32)
    a = np.empty((k // 512, 16))
    for p in range(k // 512):
        a[p, :8] = np.random.permutation(np.resize(levels, 8))
        for g in range(8):
            far = levels[np.abs(levels - a[p, g]) >= 10]
            a[p, g + 8] = far[np.random.randint(len(far))]
    return np.exp2(a.ravel()).repeat(32)


BF16 = ml_dtypes.bfloat16


def bf(x):
    return np.asarray(x, np.float32).astype(BF16)


def f64(x):
    return np.asarray(x).astype(np.float64)


B, S, DIM, HEADS = 1, 512, 2048, 16
HD = DIM // HEADS
EPS = 1e-6


def rms_norm(x, g):
    var = np.mean(np.square(x), axis=-1, keepdims=True)
    return x * (1.0 / np.sqrt(var + EPS)) * g


def rope(x, cos, sin):
    x1, x2 = np.split(x, 2, axis=-1)
    rot = np.concatenate([-x2, x1], axis=-1)
    return x * cos[None, :, None, :] + rot * sin[None, :, None, :]


def setup_inputs():
    s = mx_kscale(DIM)
    return {
        "hidden_states": bf(np.random.standard_normal((B, S, DIM)) * s),
        "cos": bf(np.random.uniform(-1.0, 1.0, (S, HD))),
        "sin": bf(np.random.uniform(-1.0, 1.0, (S, HD))),
        "w_qk": bf(np.random.standard_normal((DIM + DIM, DIM)) / np.sqrt(DIM) / s[None, :]),
        "b_qk": bf(np.random.standard_normal(DIM + DIM) * 0.2),
        "g_q": bf(1.0 + 0.1 * np.random.standard_normal(DIM)),
        "g_k": bf(1.0 + 0.1 * np.random.standard_normal(DIM)),
    }


def reference(hidden_states, cos, sin, w_qk, b_qk, g_q, g_k):
    c, sn = f64(cos), f64(sin)
    qk = (mxq(f64(hidden_states), 2, "e5m2") @ mxq(f64(w_qk), 1, "e5m2").T) + f64(b_qk)
    q = rms_norm(qk[:, :, :DIM], f64(g_q)).reshape(B, S, HEADS, HD)
    k = rms_norm(qk[:, :, DIM:], f64(g_k)).reshape(B, S, HEADS, HD)
    return rope(q, c, sn), rope(k, c, sn)

@@ -1,0 +1,268 @@
+from contextlib import ExitStack
+
+import concourse.mybir as mybir
+from concourse.masks import make_identity
+
+S, DIM, HD = 512, 2048, 128
+EPS = 1e-6
+FLOPS = 2 * S * DIM * 2 * DIM
+
+F32 = mybir.dt.float32
+BF16 = mybir.dt.bfloat16
+U32 = mybir.dt.uint32
+U8 = mybir.dt.uint8
+FP8X4 = mybir.dt.float8_e5m2_x4
+ALU = mybir.AluOpType
+ACT = mybir.ActivationFunctionType
+
+P = 128
+BANK = 512
+PASSES = DIM // BANK
+TOKEN_TILES = S // P
+CHUNKS = 2 * DIM // BANK
+HALF_CHUNKS = CHUNKS // 2
+HEADS_PER_CHUNK = BANK // HD
+HALF_HD = HD // 2
+RAW_BUFS = 12
+TAIL_CHUNKS = 2
+
+
+def tile_dynamicselfattention_pa_kernel(tc, hidden_states, cos, sin, w_qk, b_qk, g_q, g_k, out_0, out_1):
+    nc = tc.nc
+    x = hidden_states.rearrange("b s k -> (b s) k")
+    outs = [o.rearrange("b s h d -> (b s) (h d)") for o in (out_0, out_1)]
+
+    pieces = [("x", 0)] + [("w", 0, g) for g in range(PASSES)] + [("x", t) for t in range(1, TOKEN_TILES)]
+    pieces += [("w", c, g) for c in range(1, CHUNKS) for g in range(PASSES)]
+    pieces[7], pieces[8] = pieces[8], pieces[7]
+    units = [(c, t) for c in range(CHUNKS - TAIL_CHUNKS) for t in range(TOKEN_TILES)]
+    units += [(c, t) for t in range(TOKEN_TILES) for c in range(CHUNKS - TAIL_CHUNKS, CHUNKS)]
+    n_units = len(units)
+
+    def pieces_done_after(tick):
+        if tick < TOKEN_TILES:
+            return 6 + 2 * tick
+        last = (CHUNKS - TAIL_CHUNKS) * TOKEN_TILES
+        return min(len(pieces), 12 - (-(len(pieces) - 12) * (tick - 3) // (last - 3)))
+
+    with ExitStack() as ctx:
+        keep = ctx.enter_context(tc.tile_pool(name="keep", bufs=1))
+        ring = ctx.enter_context(tc.tile_pool(name="ring", bufs=3))
+        psum = ctx.enter_context(tc.psum_pool(name="psum", bufs=2))
+        ctx.enter_context(tc.manual_schedule())
+
+        raw = {}
+        grouped = {}
+        w_codes = {}
+        w_scales = {}
+        acc = {}
+        gained = {}
+        crossed = {}
+        gain_bank = {}
+        bias = {}
+
+        def load(s):
+            piece = pieces[s]
+            tile = ring.tile([P, 4, BANK], BF16, name="raw", tag="raw", bufs=RAW_BUFS)
+            if piece[0] == "x":
+                t = piece[1]
+                src = x[t * P:(t + 1) * P, :].rearrange("p (g k) -> p g k", g=PASSES)
+            else:
+                c, g = piece[1], piece[2]
+                src = w_qk[c * BANK:(c + 1) * BANK, g * BANK:(g + 1) * BANK].rearrange("(j p) k -> p j k", p=P)
+            nc.sync.dma_start(out=tile[:], in_=src)
+            raw[s] = tile
+
+        for s in range(PASSES + 1):
+            load(s)
+
+        ident = keep.tile([P, P], F32, name="ident")
+        make_identity(nc, ident[:])
+        ident_bf = keep.tile([P, P], BF16, name="ident_bf")
+        make_identity(nc, ident_bf[:])
+        minus_half = keep.tile([P, 1], F32, name="minus_half")
+        nc.gpsimd.memset(minus_half[:], -0.5)
+
+        rows = keep.tile([P, BANK], BF16, name="rows")
+        nc.vector.memset(rows[:], 0.0)
+        nc.scalar.dma_start(out=rows[0:CHUNKS, :], in_=b_qk.rearrange("(c n) -> c n", n=BANK))
+        nc.scalar.dma_start(out=rows[CHUNKS:CHUNKS + HALF_CHUNKS, :], in_=g_q.rearrange("(c n) -> c n", n=BANK))
+        nc.scalar.dma_start(out=rows[CHUNKS + HALF_CHUNKS:2 * CHUNKS, :], in_=g_k.rearrange("(c n) -> c n", n=BANK))
+
+        load(PASSES + 1)
+        cos_sb = keep.tile([P, TOKEN_TILES, HD], BF16, name="cos_sb")
+        sin_sb = keep.tile([P, TOKEN_TILES, HD], BF16, name="sin_sb")
+        nc.sync.dma_start(out=cos_sb[:], in_=cos.rearrange("(t p) d -> p t d", p=P))
+        nc.sync.dma_start(out=sin_sb[:], in_=sin.rearrange("(t p) d -> p t d", p=P))
+        for s in range(PASSES + 2, RAW_BUFS):
+            load(s)
+
+        x_codes = keep.tile([P, TOKEN_TILES, BANK], U32, name="x_codes", align_bytes=64)
+        x_scales = keep.tile([P, TOKEN_TILES, BANK], U8, name="x_scales", align_bytes=64)
+        result = keep.tile([P, TOKEN_TILES, CHUNKS, BANK], F32, name="result")
+        partial = keep.tile([P, 2, TOKEN_TILES, HALF_CHUNKS], F32, name="partial")
+        mean_eps = keep.tile([P, 2, TOKEN_TILES], F32, name="mean_eps")
+        rstd = keep.tile([P, 2, TOKEN_TILES], F32, name="rstd")
+        tables = psum.tile([P, 2, TOKEN_TILES, HD], BF16, name="tables", tag="tables", bufs=1)
+
+        def turn(s):
+            words = raw[s][:].rearrange("p j k -> p (j k)").bitcast(F32).rearrange("p (j w) -> p j w", j=4)
+            tile = ring.tile([P, 4 * BANK], BF16, name="grouped", tag="grouped", bufs=4, align_bytes=64)
+            dst = tile[:].bitcast(F32).rearrange("p (j r u) -> p j r u", j=4, u=2)
+            for b in range(2):
+                bank = psum.tile([P, 2, 2, P], F32, name="turn", tag="turn", bufs=3)
+                for jj in range(2):
+                    for u in range(2):
+                        nc.tensor.transpose(bank[:, jj, u, :], words[:, 2 * b + jj, u:2 * P:2], ident[:])
+                nc.scalar.copy(out=dst[:, 2 * b:2 * b + 2], in_=bank[:].rearrange("p j u r -> p j r u"))
+            grouped[s] = tile
+            if s + RAW_BUFS < len(pieces):
+                load(s + RAW_BUFS)
+
+        def quantize(s):
+            piece = pieces[s]
+            if piece[0] == "x":
+                codes, scales = x_codes[:, piece[1], :], x_scales[:, piece[1], :]
+            else:
+                c, g = piece[1], piece[2]
+                if g == 0:
+                    w_codes[c] = ring.tile([P, PASSES, BANK], U32, name="w_codes", tag="w_codes", bufs=4, align_bytes=64)
+                    w_scales[c] = ring.tile([P, PASSES, BANK], U8, name="w_scales", tag="w_scales", bufs=4, align_bytes=64)
+                codes, scales = w_codes[c][:, g, :], w_scales[c][:, g, :]
+            nc.vector.quantize_mx(out=codes.bitcast(FP8X4), scales=scales, in_=grouped[s][:])
+
+        def spread(dst, row):
+            nc.tensor.matmul(dst, lhsT=ident_bf[:, row:row + 1].to_broadcast([P, P]), rhs=rows[:], start=True, stop=True)
+
+        def spread_pair(pair):
+            bank = psum.tile([P, 2, BANK], BF16, name="bias_bank", tag="turn", bufs=3)
+            gain_bank[pair] = psum.tile([P, 2, BANK], BF16, name="gain_bank", tag="gain", bufs=2)
+            for i in range(2):
+                spread(bank[:, i, :], 2 * pair + i)
+            for i in range(2):
+                spread(gain_bank[pair][:, i, :], CHUNKS + 2 * pair + i)
+            bias[pair] = ring.tile([P, 2, BANK], BF16, name="bias", tag="bias", bufs=2)
+            nc.scalar.copy(out=bias[pair][:], in_=bank[:])
+
+        def fill_tables():
+            nc.scalar.activation(out=sin_sb[:, :, :HALF_HD], in_=sin_sb[:, :, :HALF_HD], func=ACT.Copy, scale=-1.0)
+            for i, src in enumerate((cos_sb, sin_sb)):
+                nc.tensor.matmul(tables[:, i].rearrange("p t d -> p (t d)"), lhsT=ident_bf[:],
+                                 rhs=src[:].rearrange("p t d -> p (t d)"), start=True, stop=True)
+
+        def multiply(i):
+            c, t = units[i]
+            acc[i] = psum.tile([P, BANK], F32, name="acc", tag="acc", bufs=2)
+            for g in range(PASSES):
+                cols = slice(g * P, (g + 1) * P)
+                nc.tensor.matmul_mx(
+                    out=acc[i][:],
+                    lhsT=x_codes[:, t, cols].bitcast(FP8X4), lhsT_scale=x_scales[:, t, cols],
+                    rhs=w_codes[c][:, g, :].bitcast(FP8X4), rhs_scale=w_scales[c][:, g, :],
+                    start=(g == 0), stop=(g == PASSES - 1))
+
+        def closes_half(i):
+            return units[i][0] % HALF_CHUNKS == HALF_CHUNKS - 1
+
+        def add_bias(i):
+            c, t = units[i]
+            half = c // HALF_CHUNKS
+            z = result[:, t, c, :]
+            nc.vector.tensor_tensor(out=z, in0=acc[i][:], in1=bias[c // 2][:, c % 2, :], op=ALU.add)
+            squares = ring.tile([P, BANK], F32, name="squares", tag="squares", bufs=2)
+            nc.scalar.activation(out=squares[:], in_=z, func=ACT.Square,
+                                 accum_out=partial[:, half, t, c % HALF_CHUNKS:c % HALF_CHUNKS + 1])
+            if closes_half(i):
+                shares = ring.tile([P, HALF_CHUNKS], F32, name="shares", tag="shares", bufs=2)
+                nc.scalar.activation(out=shares[:], in_=partial[:, half, t, :], func=ACT.Identity,
+                                     scale=1.0 / DIM, bias=EPS / HALF_CHUNKS, accum_out=mean_eps[:, half, t:t + 1])
+                nc.gpsimd.tensor_tensor(out=rstd[:, half, t:t + 1], in0=mean_eps[:, half, t:t + 1],
+                                        in1=minus_half[:], op=ALU.pow)
+
+        def apply_gain(i):
+            c, t = units[i]
+            gained[i] = ring.tile([P, HEADS_PER_CHUNK, HD], F32, name="gained", tag="gained", bufs=4)
+            dst = gained[i][:].rearrange("p h d -> p (h d)")
+            gain = gain_bank[c // 2][:, c % 2, :]
+            if closes_half(i):
+                nc.vector.scalar_tensor_tensor(out=dst, in0=result[:, t, c, :], scalar=rstd[:, c // HALF_CHUNKS, t:t + 1],
+                                               in1=gain, op0=ALU.mult, op1=ALU.mult)
+            else:
+                nc.vector.tensor_tensor(out=dst, in0=result[:, t, c, :], in1=gain, op=ALU.mult)
+
+        def per_head(table):
+            return table.unsqueeze(1).to_broadcast([P, HEADS_PER_CHUNK, table.shape[1]])
+
+        def cos_term(i):
+            c, t = units[i]
+            nc.vector.tensor_tensor(out=result[:, t, c, :].rearrange("p (h d) -> p h d", d=HD), in0=gained[i][:],
+                                    in1=per_head(tables[:, 0, t, :]), op=ALU.mult)
+
+        def sin_term(i):
+            t = units[i][1]
+            crossed[i] = ring.tile([P, HEADS_PER_CHUNK, HD], F32, name="crossed", tag="crossed", bufs=3)
+            swapped = gained[i][:].rearrange("p h (two d) -> p h two d", two=2)[:, :, ::-1, :]
+            signed_sin = tables[:, 1, t, :].rearrange("p (two d) -> p two d", two=2).unsqueeze(1)
+            nc.vector.tensor_tensor(out=crossed[i][:].rearrange("p h (two d) -> p h two d", two=2), in0=swapped,
+                                    in1=signed_sin.to_broadcast([P, HEADS_PER_CHUNK, 2, HALF_HD]), op=ALU.mult)
+
+        def store(i):
+            c, t = units[i]
+            cols = slice((c % HALF_CHUNKS) * BANK, (c % HALF_CHUNKS + 1) * BANK)
+            nc.sync.dma_start(out=outs[c // HALF_CHUNKS][t * P:(t + 1) * P, cols], in_=result[:, t, c, :])
+
+        def join(i):
+            c, t = units[i]
+            engine = nc.vector if i == n_units - 1 else nc.gpsimd
+            engine.tensor_tensor(out=result[:, t, c, :], in0=result[:, t, c, :],
+                                 in1=crossed[i][:].rearrange("p h d -> p (h d)"), op=ALU.add)
+            if closes_half(i):
+                store(i)
+
+        def normalise(i):
+            c, t = units[i]
+            nc.scalar.activation(out=result[:, t, c, :], in_=result[:, t, c, :], func=ACT.Copy,
+                                 scale=rstd[:, c // HALF_CHUNKS, t:t + 1])
+            store(i)
+
+        def ready_tick(i):
+            c, t = units[i]
+            closer = units.index((c - c % HALF_CHUNKS + HALF_CHUNKS - 1, t))
+            return max(i + 5, closer + 2)
+
+        waiting = sorted((i for i in range(n_units) if not closes_half(i)), key=lambda i: (ready_tick(i), i))
+
+        done = PASSES + 1
+        for s in range(done):
+            turn(s)
+            quantize(s)
+        spread_pair(0)
+
+        for tick in range(n_units + 5):
+            fresh = range(done, pieces_done_after(tick))
+            for s in fresh:
+                turn(s)
+            done = fresh.stop
+            if tick == 1:
+                fill_tables()
+            if tick % 8 == 5 and tick // 8 + 1 < CHUNKS // 2:
+                spread_pair(tick // 8 + 1)
+            if tick < n_units:
+                multiply(tick)
+            if 0 <= tick - 4 < n_units:
+                sin_term(tick - 4)
+                join(tick - 4)
+            if 0 <= tick - 1 < n_units:
+                add_bias(tick - 1)
+            if 0 <= tick - 2 < n_units:
+                apply_gain(tick - 2)
+            if 0 <= tick - 3 < n_units:
+                cos_term(tick - 3)
+            for s in fresh:
+                quantize(s)
+            for turn_no in range(1 if len(fresh) else 2):
+                if waiting and ready_tick(waiting[0]) <= tick:
+                    first = waiting[0]
+                    waiting.remove(first)
+                    normalise(first)
+        assert not waiting

@@ -23,27 +23,29 @@ CHUNKS = 2 * DIM // BANK
 HALF_CHUNKS = CHUNKS // 2
 HEADS_PER_CHUNK = BANK // HD
 HALF_HD = HD // 2
-RAW_BUFS = 12
-TAIL_CHUNKS = 2
+RAW_BUFS = 10
+HEAD_PIECES = PASSES + 2
+REORDERED = 8
+GPSIMD_HEADS = 1
+DOUBLE_STEPS = (4, 8)
+NORMALISED_PER_STEP = 3
 
 
 def tile_dynamicselfattention_pa_kernel(tc, hidden_states, cos, sin, w_qk, b_qk, g_q, g_k, out_0, out_1):
     nc = tc.nc
-    x = hidden_states.rearrange("b s k -> (b s) k")
-    outs = [o.rearrange("b s h d -> (b s) (h d)") for o in (out_0, out_1)]
+    x = hidden_states.rearrange("b (p t) k -> (b t) p k", t=TOKEN_TILES)
+    outs = [o.rearrange("b (p t) h d -> (b t) p (h d)", t=TOKEN_TILES) for o in (out_0, out_1)]
 
     pieces = [("x", 0)] + [("w", 0, g) for g in range(PASSES)] + [("x", t) for t in range(1, TOKEN_TILES)]
     pieces += [("w", c, g) for c in range(1, CHUNKS) for g in range(PASSES)]
-    pieces[7], pieces[8] = pieces[8], pieces[7]
-    units = [(c, t) for c in range(CHUNKS - TAIL_CHUNKS) for t in range(TOKEN_TILES)]
-    units += [(c, t) for t in range(TOKEN_TILES) for c in range(CHUNKS - TAIL_CHUNKS, CHUNKS)]
-    n_units = len(units)
+    n_pairs = CHUNKS * TOKEN_TILES // 2
 
-    def pieces_done_after(tick):
-        if tick < TOKEN_TILES:
-            return 6 + 2 * tick
-        last = (CHUNKS - TAIL_CHUNKS) * TOKEN_TILES
-        return min(len(pieces), 12 - (-(len(pieces) - 12) * (tick - 3) // (last - 3)))
+    token_pairs = (CHUNKS - 2) * TOKEN_TILES // 2
+
+    def units_of(p):
+        if p < token_pairs:
+            return [(p // 2, 2 * (p % 2) + i) for i in range(2)]
+        return [(CHUNKS - 2 + i, p - token_pairs) for i in range(2)]
 
     with ExitStack() as ctx:
         keep = ctx.enter_context(tc.tile_pool(name="keep", bufs=1))
@@ -52,6 +54,7 @@ def tile_dynamicselfattention_pa_kernel(tc, hidden_states, cos, sin, w_qk, b_qk,
         ctx.enter_context(tc.manual_schedule())
 
         raw = {}
+        ordered = {}
         grouped = {}
         w_codes = {}
         w_scales = {}
@@ -66,7 +69,7 @@ def tile_dynamicselfattention_pa_kernel(tc, hidden_states, cos, sin, w_qk, b_qk,
             tile = ring.tile([P, 4, BANK], BF16, name="raw", tag="raw", bufs=RAW_BUFS)
             if piece[0] == "x":
                 t = piece[1]
-                src = x[t * P:(t + 1) * P, :].rearrange("p (g k) -> p g k", g=PASSES)
+                src = x[t].rearrange("p (g k) -> p g k", g=PASSES)
             else:
                 c, g = piece[1], piece[2]
                 src = w_qk[c * BANK:(c + 1) * BANK, g * BANK:(g + 1) * BANK].rearrange("(j p) k -> p j k", p=P)
@@ -80,7 +83,7 @@ def tile_dynamicselfattention_pa_kernel(tc, hidden_states, cos, sin, w_qk, b_qk,
         make_identity(nc, ident[:])
         ident_bf = keep.tile([P, P], BF16, name="ident_bf")
         make_identity(nc, ident_bf[:])
-        minus_half = keep.tile([P, 1], F32, name="minus_half")
+        minus_half = keep.tile([P, 2], F32, name="minus_half")
         nc.gpsimd.memset(minus_half[:], -0.5)
 
         rows = keep.tile([P, BANK], BF16, name="rows")
@@ -92,8 +95,8 @@ def tile_dynamicselfattention_pa_kernel(tc, hidden_states, cos, sin, w_qk, b_qk,
         load(PASSES + 1)
         cos_sb = keep.tile([P, TOKEN_TILES, HD], BF16, name="cos_sb")
         sin_sb = keep.tile([P, TOKEN_TILES, HD], BF16, name="sin_sb")
-        nc.sync.dma_start(out=cos_sb[:], in_=cos.rearrange("(t p) d -> p t d", p=P))
-        nc.sync.dma_start(out=sin_sb[:], in_=sin.rearrange("(t p) d -> p t d", p=P))
+        nc.sync.dma_start(out=cos_sb[:], in_=cos.rearrange("(p t) d -> p t d", p=P))
+        nc.sync.dma_start(out=sin_sb[:], in_=sin.rearrange("(p t) d -> p t d", p=P))
         for s in range(PASSES + 2, RAW_BUFS):
             load(s)
 
@@ -105,44 +108,61 @@ def tile_dynamicselfattention_pa_kernel(tc, hidden_states, cos, sin, w_qk, b_qk,
         rstd = keep.tile([P, 2, TOKEN_TILES], F32, name="rstd")
         tables = psum.tile([P, 2, TOKEN_TILES, HD], BF16, name="tables", tag="tables", bufs=1)
 
+        def reorder(s):
+            words = raw[s][:].rearrange("p j k -> p (j k)").bitcast(F32)
+            ordered[s] = ring.tile([P, 4, 2, P], F32, name="ordered", tag="ordered", bufs=2)
+            nc.vector.tensor_copy(out=ordered[s][:], in_=words.rearrange("p (j w u) -> p j u w", j=4, u=2))
+            if s + RAW_BUFS < len(pieces):
+                load(s + RAW_BUFS)
+
         def turn(s):
+            if s < HEAD_PIECES or s % 2 == 0:
+                grouped[s] = ring.tile([P, 2, 4 * BANK], BF16, name="grouped", tag="grouped", bufs=4, align_bytes=64)
+                tile, slot = grouped[s], 0
+            else:
+                tile, slot = grouped[s - 1], 1
+            dst = tile[:, slot, :].bitcast(F32).rearrange("p (j r u) -> p j r u", j=4, u=2)
             words = raw[s][:].rearrange("p j k -> p (j k)").bitcast(F32).rearrange("p (j w) -> p j w", j=4)
-            tile = ring.tile([P, 4 * BANK], BF16, name="grouped", tag="grouped", bufs=4, align_bytes=64)
-            dst = tile[:].bitcast(F32).rearrange("p (j r u) -> p j r u", j=4, u=2)
             for b in range(2):
                 bank = psum.tile([P, 2, 2, P], F32, name="turn", tag="turn", bufs=3)
                 for jj in range(2):
                     for u in range(2):
-                        nc.tensor.transpose(bank[:, jj, u, :], words[:, 2 * b + jj, u:2 * P:2], ident[:])
+                        j = 2 * b + jj
+                        src = ordered[s][:, j, u, :] if s < REORDERED else words[:, j, u:2 * P:2]
+                        nc.tensor.transpose(bank[:, jj, u, :], src, ident[:])
                 nc.scalar.copy(out=dst[:, 2 * b:2 * b + 2], in_=bank[:].rearrange("p j u r -> p j r u"))
-            grouped[s] = tile
-            if s + RAW_BUFS < len(pieces):
+            if s >= REORDERED and s + RAW_BUFS < len(pieces):
                 load(s + RAW_BUFS)
 
-        def quantize(s):
+        def quantize(s, count):
             piece = pieces[s]
             if piece[0] == "x":
-                codes, scales = x_codes[:, piece[1], :], x_scales[:, piece[1], :]
+                t = piece[1]
+                codes, scales = x_codes[:, t:t + count, :], x_scales[:, t:t + count, :]
             else:
                 c, g = piece[1], piece[2]
                 if g == 0:
-                    w_codes[c] = ring.tile([P, PASSES, BANK], U32, name="w_codes", tag="w_codes", bufs=4, align_bytes=64)
-                    w_scales[c] = ring.tile([P, PASSES, BANK], U8, name="w_scales", tag="w_scales", bufs=4, align_bytes=64)
-                codes, scales = w_codes[c][:, g, :], w_scales[c][:, g, :]
-            nc.vector.quantize_mx(out=codes.bitcast(FP8X4), scales=scales, in_=grouped[s][:])
+                    w_codes[c] = ring.tile([P, PASSES, BANK], U32, name="w_codes", tag="w_codes", bufs=3, align_bytes=64)
+                    w_scales[c] = ring.tile([P, PASSES, BANK], U8, name="w_scales", tag="w_scales", bufs=3, align_bytes=64)
+                codes, scales = w_codes[c][:, g:g + count, :], w_scales[c][:, g:g + count, :]
+            nc.vector.quantize_mx(out=codes.rearrange("p a n -> p (a n)").bitcast(FP8X4),
+                                  scales=scales.rearrange("p a n -> p (a n)"),
+                                  in_=grouped[s][:, 0:count, :].rearrange("p a n -> p (a n)"))
 
         def spread(dst, row):
             nc.tensor.matmul(dst, lhsT=ident_bf[:, row:row + 1].to_broadcast([P, P]), rhs=rows[:], start=True, stop=True)
 
-        def spread_pair(pair):
+        def spread_bias(group):
             bank = psum.tile([P, 2, BANK], BF16, name="bias_bank", tag="turn", bufs=3)
-            gain_bank[pair] = psum.tile([P, 2, BANK], BF16, name="gain_bank", tag="gain", bufs=2)
             for i in range(2):
-                spread(bank[:, i, :], 2 * pair + i)
-            for i in range(2):
-                spread(gain_bank[pair][:, i, :], CHUNKS + 2 * pair + i)
-            bias[pair] = ring.tile([P, 2, BANK], BF16, name="bias", tag="bias", bufs=2)
-            nc.scalar.copy(out=bias[pair][:], in_=bank[:])
+                spread(bank[:, i, :], 2 * group + i)
+            bias[group] = ring.tile([P, 2, BANK], BF16, name="bias", tag="bias", bufs=2)
+            nc.scalar.copy(out=bias[group][:], in_=bank[:])
+
+        def spread_gain(c):
+            if c % 2 == 0:
+                gain_bank[c // 2] = psum.tile([P, 2, BANK], BF16, name="gain_bank", tag="gain", bufs=2)
+            spread(gain_bank[c // 2][:, c % 2, :], CHUNKS + c)
 
         def fill_tables():
             nc.scalar.activation(out=sin_sb[:, :, :HALF_HD], in_=sin_sb[:, :, :HALF_HD], func=ACT.Copy, scale=-1.0)
@@ -150,119 +170,192 @@ def tile_dynamicselfattention_pa_kernel(tc, hidden_states, cos, sin, w_qk, b_qk,
                 nc.tensor.matmul(tables[:, i].rearrange("p t d -> p (t d)"), lhsT=ident_bf[:],
                                  rhs=src[:].rearrange("p t d -> p (t d)"), start=True, stop=True)
 
-        def multiply(i):
-            c, t = units[i]
-            acc[i] = psum.tile([P, BANK], F32, name="acc", tag="acc", bufs=2)
+        def multiply(c, t):
+            acc[c, t] = psum.tile([P, BANK], F32, name="acc", tag="acc", bufs=2)
             for g in range(PASSES):
                 cols = slice(g * P, (g + 1) * P)
                 nc.tensor.matmul_mx(
-                    out=acc[i][:],
+                    out=acc[c, t][:],
                     lhsT=x_codes[:, t, cols].bitcast(FP8X4), lhsT_scale=x_scales[:, t, cols],
                     rhs=w_codes[c][:, g, :].bitcast(FP8X4), rhs_scale=w_scales[c][:, g, :],
                     start=(g == 0), stop=(g == PASSES - 1))
 
-        def closes_half(i):
-            return units[i][0] % HALF_CHUNKS == HALF_CHUNKS - 1
+        def pair_view(p):
+            (c, t), (c_next, t_next) = units_of(p)
+            return result[:, t:t_next + 1, c:c_next + 1, :].rearrange("p t c n -> p (t c) n")
 
-        def add_bias(i):
-            c, t = units[i]
-            half = c // HALF_CHUNKS
-            z = result[:, t, c, :]
-            nc.vector.tensor_tensor(out=z, in0=acc[i][:], in1=bias[c // 2][:, c % 2, :], op=ALU.add)
-            squares = ring.tile([P, BANK], F32, name="squares", tag="squares", bufs=2)
-            nc.scalar.activation(out=squares[:], in_=z, func=ACT.Square,
-                                 accum_out=partial[:, half, t, c % HALF_CHUNKS:c % HALF_CHUNKS + 1])
-            if closes_half(i):
-                shares = ring.tile([P, HALF_CHUNKS], F32, name="shares", tag="shares", bufs=2)
-                nc.scalar.activation(out=shares[:], in_=partial[:, half, t, :], func=ACT.Identity,
-                                     scale=1.0 / DIM, bias=EPS / HALF_CHUNKS, accum_out=mean_eps[:, half, t:t + 1])
-                nc.gpsimd.tensor_tensor(out=rstd[:, half, t:t + 1], in0=mean_eps[:, half, t:t + 1],
-                                        in1=minus_half[:], op=ALU.pow)
+        def pair_table(p, table):
+            (c, t), (c_next, t_next) = units_of(p)
+            return table[:, t:t_next + 1, :].to_broadcast([P, 2, HD])
 
-        def apply_gain(i):
-            c, t = units[i]
-            gained[i] = ring.tile([P, HEADS_PER_CHUNK, HD], F32, name="gained", tag="gained", bufs=4)
-            dst = gained[i][:].rearrange("p h d -> p (h d)")
-            gain = gain_bank[c // 2][:, c % 2, :]
-            if closes_half(i):
-                nc.vector.scalar_tensor_tensor(out=dst, in0=result[:, t, c, :], scalar=rstd[:, c // HALF_CHUNKS, t:t + 1],
-                                               in1=gain, op0=ALU.mult, op1=ALU.mult)
+        def add_bias(c, t):
+            nc.vector.tensor_tensor(out=result[:, t, c, :], in0=acc[c, t][:], in1=bias[c // 2][:, c % 2, :], op=ALU.add)
+
+        def statistics(p):
+            for c, t in units_of(p):
+                squares = ring.tile([P, BANK], F32, name="squares", tag="squares", bufs=2)
+                nc.scalar.activation(out=squares[:], in_=result[:, t, c, :], func=ACT.Square,
+                                     accum_out=partial[:, c // HALF_CHUNKS, t, c % HALF_CHUNKS:c % HALF_CHUNKS + 1])
+            closed = [t for c, t in units_of(p) if c % HALF_CHUNKS == HALF_CHUNKS - 1]
+            if closed:
+                half = units_of(p)[0][0] // HALF_CHUNKS
+                for t in closed:
+                    shares = ring.tile([P, HALF_CHUNKS], F32, name="shares", tag="shares", bufs=2)
+                    nc.scalar.activation(out=shares[:], in_=partial[:, half, t, :], func=ACT.Identity,
+                                         scale=1.0 / DIM, bias=EPS / HALF_CHUNKS, accum_out=mean_eps[:, half, t:t + 1])
+                span = slice(closed[0], closed[-1] + 1)
+                nc.gpsimd.tensor_tensor(out=rstd[:, half, span], in0=mean_eps[:, half, span],
+                                        in1=minus_half[:, :len(closed)], op=ALU.pow)
+
+        def gpsimd_heads(p):
+            return 0 if p in (0, 1, 2, n_pairs - 1) else GPSIMD_HEADS
+
+        def apply_gain(p):
+            c, t = units_of(p)[0]
+            gained[p] = ring.tile([P, 2, HEADS_PER_CHUNK, HD], F32, name="gained", tag="gained", bufs=3)
+            dst = gained[p][:].rearrange("p t h d -> p t (h d)")
+            if p < token_pairs:
+                gain = gain_bank[c // 2][:, c % 2:c % 2 + 1, :].to_broadcast([P, 2, BANK])
+                nc.vector.tensor_tensor(out=dst, in0=pair_view(p), in1=gain, op=ALU.mult)
             else:
-                nc.vector.tensor_tensor(out=dst, in0=result[:, t, c, :], in1=gain, op=ALU.mult)
+                nc.vector.scalar_tensor_tensor(out=dst, in0=pair_view(p), scalar=rstd[:, 1, t:t + 1],
+                                               in1=gain_bank[c // 2][:], op0=ALU.mult, op1=ALU.mult)
 
-        def per_head(table):
-            return table.unsqueeze(1).to_broadcast([P, HEADS_PER_CHUNK, table.shape[1]])
+        def cos_on_gpsimd(p):
+            heads = gpsimd_heads(p)
+            if heads:
+                dst = pair_view(p).rearrange("p a (h d) -> p a h d", d=HD)
+                nc.gpsimd.tensor_tensor(out=dst[:, :, -heads:, :], in0=gained[p][:, :, -heads:, :],
+                                        in1=pair_table(p, cos_sb).unsqueeze(2).to_broadcast([P, 2, heads, HD]), op=ALU.mult)
 
-        def cos_term(i):
-            c, t = units[i]
-            nc.vector.tensor_tensor(out=result[:, t, c, :].rearrange("p (h d) -> p h d", d=HD), in0=gained[i][:],
-                                    in1=per_head(tables[:, 0, t, :]), op=ALU.mult)
+        def cos_term(p):
+            heads = HEADS_PER_CHUNK - gpsimd_heads(p)
+            dst = pair_view(p).rearrange("p a (h d) -> p a h d", d=HD)
+            nc.vector.tensor_tensor(out=dst[:, :, :heads, :], in0=gained[p][:, :, :heads, :],
+                                    in1=pair_table(p, tables[:, 0]).unsqueeze(2).to_broadcast([P, 2, heads, HD]), op=ALU.mult)
 
-        def sin_term(i):
-            t = units[i][1]
-            crossed[i] = ring.tile([P, HEADS_PER_CHUNK, HD], F32, name="crossed", tag="crossed", bufs=3)
-            swapped = gained[i][:].rearrange("p h (two d) -> p h two d", two=2)[:, :, ::-1, :]
-            signed_sin = tables[:, 1, t, :].rearrange("p (two d) -> p two d", two=2).unsqueeze(1)
-            nc.vector.tensor_tensor(out=crossed[i][:].rearrange("p h (two d) -> p h two d", two=2), in0=swapped,
-                                    in1=signed_sin.to_broadcast([P, HEADS_PER_CHUNK, 2, HALF_HD]), op=ALU.mult)
+        def sin_term(p):
+            crossed[p] = ring.tile([P, 2, HEADS_PER_CHUNK, 2, HALF_HD], F32, name="crossed", tag="crossed", bufs=3)
+            swapped = gained[p][:].rearrange("p a h (two d) -> p a h two d", two=2)[:, :, :, ::-1, :]
+            signed_sin = pair_table(p, tables[:, 1]).rearrange("p a (two d) -> p a two d", two=2).unsqueeze(2)
+            nc.vector.tensor_tensor(out=crossed[p][:], in0=swapped,
+                                    in1=signed_sin.to_broadcast([P, 2, HEADS_PER_CHUNK, 2, HALF_HD]), op=ALU.mult)
 
-        def store(i):
-            c, t = units[i]
+        def store(c, t):
             cols = slice((c % HALF_CHUNKS) * BANK, (c % HALF_CHUNKS + 1) * BANK)
-            nc.sync.dma_start(out=outs[c // HALF_CHUNKS][t * P:(t + 1) * P, cols], in_=result[:, t, c, :])
+            nc.sync.dma_start(out=outs[c // HALF_CHUNKS][t][:, cols], in_=result[:, t, c, :])
 
-        def join(i):
-            c, t = units[i]
-            engine = nc.vector if i == n_units - 1 else nc.gpsimd
-            engine.tensor_tensor(out=result[:, t, c, :], in0=result[:, t, c, :],
-                                 in1=crossed[i][:].rearrange("p h d -> p (h d)"), op=ALU.add)
-            if closes_half(i):
-                store(i)
+        def join(p):
+            cross = crossed[p][:].rearrange("p a h two d -> p a (h two d)")
+            if p == n_pairs - 1:
+                for i in range(2):
+                    nc.vector.tensor_tensor(out=pair_view(p)[:, i, :], in0=pair_view(p)[:, i, :], in1=cross[:, i, :], op=ALU.add)
+            else:
+                nc.gpsimd.tensor_tensor(out=pair_view(p), in0=pair_view(p), in1=cross, op=ALU.add)
 
-        def normalise(i):
-            c, t = units[i]
+        def normalise(c, t):
             nc.scalar.activation(out=result[:, t, c, :], in_=result[:, t, c, :], func=ACT.Copy,
                                  scale=rstd[:, c // HALF_CHUNKS, t:t + 1])
-            store(i)
+            store(c, t)
 
-        def ready_tick(i):
-            c, t = units[i]
-            closer = units.index((c - c % HALF_CHUNKS + HALF_CHUNKS - 1, t))
-            return max(i + 5, closer + 2)
+        def ready_step(p, t):
+            if p < n_pairs // 2:
+                return max(p + 3, n_pairs // 2 + t // 2)
+            return token_pairs + t + 1
 
-        waiting = sorted((i for i in range(n_units) if not closes_half(i)), key=lambda i: (ready_tick(i), i))
+        waiting = sorted((ready_step(p, t), t, c) for p in range(token_pairs) for c, t in units_of(p))
 
-        done = PASSES + 1
-        for s in range(done):
+        spread_bias(0)
+        spread_gain(0)
+        spread_gain(1)
+        for s in range(HEAD_PIECES):
+            reorder(s)
             turn(s)
-            quantize(s)
-        spread_pair(0)
+            if s >= 2:
+                quantize(s - 2, 1)
+        quantize(4, 1)
+        multiply(0, 0)
+        reorder(6)
+        quantize(5, 1)
+        turn(6)
+        multiply(0, 1)
+        fill_tables()
+        reorder(7)
+        turn(7)
+        add_bias(0, 0)
+        add_bias(0, 1)
+        quantize(6, 2)
+        turn(8)
+        turn(9)
+        statistics(0)
+        multiply(0, 2)
+        turn(10)
+        turn(11)
+        multiply(0, 3)
+        turn(12)
+        turn(13)
+        spread_bias(1)
+        apply_gain(0)
+        quantize(8, 2)
+        cos_term(0)
+        add_bias(0, 2)
+        sin_term(0)
+        quantize(10, 2)
+        join(0)
+        add_bias(0, 3)
+        statistics(1)
 
-        for tick in range(n_units + 5):
-            fresh = range(done, pieces_done_after(tick))
-            for s in fresh:
-                turn(s)
-            done = fresh.stop
-            if tick == 1:
-                fill_tables()
-            if tick % 8 == 5 and tick // 8 + 1 < CHUNKS // 2:
-                spread_pair(tick // 8 + 1)
-            if tick < n_units:
-                multiply(tick)
-            if 0 <= tick - 4 < n_units:
-                sin_term(tick - 4)
-                join(tick - 4)
-            if 0 <= tick - 1 < n_units:
-                add_bias(tick - 1)
-            if 0 <= tick - 2 < n_units:
-                apply_gain(tick - 2)
-            if 0 <= tick - 3 < n_units:
-                cos_term(tick - 3)
-            for s in fresh:
-                quantize(s)
-            for turn_no in range(1 if len(fresh) else 2):
-                if waiting and ready_tick(waiting[0]) <= tick:
-                    first = waiting[0]
-                    waiting.remove(first)
-                    normalise(first)
+        done = 14
+        unquantized = [12]
+        for step in range(2, n_pairs + 3):
+            runs = [] if done == len(pieces) else [done, done + 2] if step in DOUBLE_STEPS else [done]
+            done += 2 * len(runs)
+            late = step - 2 if 5 <= step < n_pairs + 2 else None
+            if token_pairs <= step - 3:
+                for c, t in units_of(step - 3):
+                    store(c, t)
+            if step == 3:
+                sin_term(1)
+                join(1)
+            if step == 4:
+                cos_term(2)
+            if late and unquantized:
+                apply_gain(late)
+            if 3 <= step <= n_pairs:
+                add_bias(*units_of(step - 1)[0])
+            if late and not unquantized:
+                apply_gain(late)
+            if late:
+                cos_on_gpsimd(late)
+            if 3 <= step <= n_pairs:
+                add_bias(*units_of(step - 1)[1])
+                statistics(step - 1)
+            if step in (2, 3):
+                apply_gain(step - 1)
+            group = step // 4 + 1
+            if group < CHUNKS // 2:
+                if step % 4 == 1:
+                    spread_bias(group)
+                if step % 4 >= 2:
+                    spread_gain(2 * group + step % 2)
+            if step < n_pairs:
+                for i in range(2):
+                    multiply(*units_of(step)[i])
+                    for s in range(done - (2 - i) * len(runs), done - (1 - i) * len(runs)):
+                        turn(s)
+            if step == 2:
+                cos_term(1)
+            if late:
+                cos_term(late)
+            if 4 <= step < n_pairs + 2:
+                sin_term(step - 2)
+            for first in unquantized:
+                quantize(first, 2)
+            unquantized = runs
+            if 4 <= step < n_pairs + 2:
+                join(step - 2)
+            for ready, t, c in waiting[:NORMALISED_PER_STEP]:
+                if ready <= step:
+                    waiting.remove((ready, t, c))
+                    normalise(c, t)
         assert not waiting

@@ -25,8 +25,9 @@ HEADS_PER_CHUNK = BANK // HD
 HALF_HD = HD // 2
 RAW_BUFS = 10
 HEAD_PIECES = PASSES + 2
-REORDERED = 8
-GPSIMD_HEADS = 1
+FIRST_FUSED_PAIR = 10
+FIRST_FUSED_CHUNK = FIRST_FUSED_PAIR // 2
+FUSED_HEADS = (CHUNKS - FIRST_FUSED_CHUNK) * HEADS_PER_CHUNK
 DOUBLE_STEPS = (4, 8)
 NORMALISED_PER_STEP = 3
 
@@ -54,7 +55,9 @@ def tile_dynamicselfattention_pa_kernel(tc, hidden_states, cos, sin, w_qk, b_qk,
         ctx.enter_context(tc.manual_schedule())
 
         raw = {}
-        ordered = {}
+        consumed = set()
+        gain_cos = {}
+        gain_sin = {}
         grouped = {}
         w_codes = {}
         w_scales = {}
@@ -76,7 +79,13 @@ def tile_dynamicselfattention_pa_kernel(tc, hidden_states, cos, sin, w_qk, b_qk,
             nc.sync.dma_start(out=tile[:], in_=src)
             raw[s] = tile
 
-        for s in range(PASSES + 1):
+        rows = keep.tile([P, BANK], BF16, name="rows")
+        nc.vector.memset(rows[:], 0.0)
+        load(0)
+        nc.sync.dma_start(out=rows[0:CHUNKS, :], in_=b_qk.rearrange("(c n) -> c n", n=BANK))
+        nc.sync.dma_start(out=rows[CHUNKS:CHUNKS + HALF_CHUNKS, :], in_=g_q.rearrange("(c n) -> c n", n=BANK))
+        nc.sync.dma_start(out=rows[CHUNKS + HALF_CHUNKS:2 * CHUNKS, :], in_=g_k.rearrange("(c n) -> c n", n=BANK))
+        for s in range(1, PASSES + 1):
             load(s)
 
         ident = keep.tile([P, P], F32, name="ident")
@@ -86,12 +95,6 @@ def tile_dynamicselfattention_pa_kernel(tc, hidden_states, cos, sin, w_qk, b_qk,
         minus_half = keep.tile([P, 2], F32, name="minus_half")
         nc.gpsimd.memset(minus_half[:], -0.5)
 
-        rows = keep.tile([P, BANK], BF16, name="rows")
-        nc.vector.memset(rows[:], 0.0)
-        nc.scalar.dma_start(out=rows[0:CHUNKS, :], in_=b_qk.rearrange("(c n) -> c n", n=BANK))
-        nc.scalar.dma_start(out=rows[CHUNKS:CHUNKS + HALF_CHUNKS, :], in_=g_q.rearrange("(c n) -> c n", n=BANK))
-        nc.scalar.dma_start(out=rows[CHUNKS + HALF_CHUNKS:2 * CHUNKS, :], in_=g_k.rearrange("(c n) -> c n", n=BANK))
-
         load(PASSES + 1)
         cos_sb = keep.tile([P, TOKEN_TILES, HD], BF16, name="cos_sb")
         sin_sb = keep.tile([P, TOKEN_TILES, HD], BF16, name="sin_sb")
@@ -100,6 +103,12 @@ def tile_dynamicselfattention_pa_kernel(tc, hidden_states, cos, sin, w_qk, b_qk,
         for s in range(PASSES + 2, RAW_BUFS):
             load(s)
 
+        head_rows = keep.tile([P, HD], BF16, name="head_rows")
+        nc.gpsimd.memset(head_rows[:], 0.0)
+        sin_swapped = keep.tile([P, TOKEN_TILES, 2, HALF_HD], BF16, name="sin_swapped")
+        rope_t = keep.tile([P, 2, TOKEN_TILES, P], BF16, name="rope_t")
+        gain_columns = keep.tile([P, FUSED_HEADS], F32, name="gain_columns")
+        diagonals = keep.tile([P, FUSED_HEADS, HD], BF16, name="diagonals")
         x_codes = keep.tile([P, TOKEN_TILES, BANK], U32, name="x_codes", align_bytes=64)
         x_scales = keep.tile([P, TOKEN_TILES, BANK], U8, name="x_scales", align_bytes=64)
         result = keep.tile([P, TOKEN_TILES, CHUNKS, BANK], F32, name="result")
@@ -108,12 +117,10 @@ def tile_dynamicselfattention_pa_kernel(tc, hidden_states, cos, sin, w_qk, b_qk,
         rstd = keep.tile([P, 2, TOKEN_TILES], F32, name="rstd")
         tables = psum.tile([P, 2, TOKEN_TILES, HD], BF16, name="tables", tag="tables", bufs=1)
 
-        def reorder(s):
-            words = raw[s][:].rearrange("p j k -> p (j k)").bitcast(F32)
-            ordered[s] = ring.tile([P, 4, 2, P], F32, name="ordered", tag="ordered", bufs=2)
-            nc.vector.tensor_copy(out=ordered[s][:], in_=words.rearrange("p (j w u) -> p j u w", j=4, u=2))
-            if s + RAW_BUFS < len(pieces):
-                load(s + RAW_BUFS)
+        def release(s):
+            consumed.add(s)
+            while len(raw) < len(pieces) and len(raw) - RAW_BUFS in consumed:
+                load(len(raw))
 
         def turn(s):
             if s < HEAD_PIECES or s % 2 == 0:
@@ -128,11 +135,9 @@ def tile_dynamicselfattention_pa_kernel(tc, hidden_states, cos, sin, w_qk, b_qk,
                 for jj in range(2):
                     for u in range(2):
                         j = 2 * b + jj
-                        src = ordered[s][:, j, u, :] if s < REORDERED else words[:, j, u:2 * P:2]
-                        nc.tensor.transpose(bank[:, jj, u, :], src, ident[:])
+                        nc.tensor.transpose(bank[:, jj, u, :], words[:, j, u:2 * P:2], ident[:])
                 nc.scalar.copy(out=dst[:, 2 * b:2 * b + 2], in_=bank[:].rearrange("p j u r -> p j r u"))
-            if s >= REORDERED and s + RAW_BUFS < len(pieces):
-                load(s + RAW_BUFS)
+            release(s)
 
         def quantize(s, count):
             piece = pieces[s]
@@ -207,32 +212,16 @@ def tile_dynamicselfattention_pa_kernel(tc, hidden_states, cos, sin, w_qk, b_qk,
                 nc.gpsimd.tensor_tensor(out=rstd[:, half, span], in0=mean_eps[:, half, span],
                                         in1=minus_half[:, :len(closed)], op=ALU.pow)
 
-        def gpsimd_heads(p):
-            return 0 if p in (0, 1, 2, n_pairs - 1) else GPSIMD_HEADS
-
         def apply_gain(p):
-            c, t = units_of(p)[0]
+            c = units_of(p)[0][0]
             gained[p] = ring.tile([P, 2, HEADS_PER_CHUNK, HD], F32, name="gained", tag="gained", bufs=3)
             dst = gained[p][:].rearrange("p t h d -> p t (h d)")
-            if p < token_pairs:
-                gain = gain_bank[c // 2][:, c % 2:c % 2 + 1, :].to_broadcast([P, 2, BANK])
-                nc.vector.tensor_tensor(out=dst, in0=pair_view(p), in1=gain, op=ALU.mult)
-            else:
-                nc.vector.scalar_tensor_tensor(out=dst, in0=pair_view(p), scalar=rstd[:, 1, t:t + 1],
-                                               in1=gain_bank[c // 2][:], op0=ALU.mult, op1=ALU.mult)
-
-        def cos_on_gpsimd(p):
-            heads = gpsimd_heads(p)
-            if heads:
-                dst = pair_view(p).rearrange("p a (h d) -> p a h d", d=HD)
-                nc.gpsimd.tensor_tensor(out=dst[:, :, -heads:, :], in0=gained[p][:, :, -heads:, :],
-                                        in1=pair_table(p, cos_sb).unsqueeze(2).to_broadcast([P, 2, heads, HD]), op=ALU.mult)
+            gain = gain_bank[c // 2][:, c % 2:c % 2 + 1, :].to_broadcast([P, 2, BANK])
+            nc.vector.tensor_tensor(out=dst, in0=pair_view(p), in1=gain, op=ALU.mult)
 
         def cos_term(p):
-            heads = HEADS_PER_CHUNK - gpsimd_heads(p)
-            dst = pair_view(p).rearrange("p a (h d) -> p a h d", d=HD)
-            nc.vector.tensor_tensor(out=dst[:, :, :heads, :], in0=gained[p][:, :, :heads, :],
-                                    in1=pair_table(p, tables[:, 0]).unsqueeze(2).to_broadcast([P, 2, heads, HD]), op=ALU.mult)
+            table = pair_table(p, tables[:, 0]).unsqueeze(2).to_broadcast([P, 2, HEADS_PER_CHUNK, HD])
+            nc.vector.tensor_tensor(out=pair_view(p).rearrange("p a (h d) -> p a h d", d=HD), in0=gained[p][:], in1=table, op=ALU.mult)
 
         def sin_term(p):
             crossed[p] = ring.tile([P, 2, HEADS_PER_CHUNK, 2, HALF_HD], F32, name="crossed", tag="crossed", bufs=3)
@@ -240,6 +229,45 @@ def tile_dynamicselfattention_pa_kernel(tc, hidden_states, cos, sin, w_qk, b_qk,
             signed_sin = pair_table(p, tables[:, 1]).rearrange("p a (two d) -> p a two d", two=2).unsqueeze(2)
             nc.vector.tensor_tensor(out=crossed[p][:], in0=swapped,
                                     in1=signed_sin.to_broadcast([P, 2, HEADS_PER_CHUNK, 2, HALF_HD]), op=ALU.mult)
+
+        def prepare_fused():
+            nc.scalar.copy(out=sin_swapped[:], in_=sin_sb[:].rearrange("p t (two d) -> p t two d", two=2)[:, :, ::-1, :])
+            bank = psum.tile([P, 2, TOKEN_TILES, P], BF16, name="rope_turn", tag="turn", bufs=3)
+            for t in range(TOKEN_TILES):
+                nc.tensor.transpose(bank[:, 0, t, :], cos_sb[:, t, :], ident_bf[:])
+                nc.tensor.transpose(bank[:, 1, t, :], sin_swapped[:, t].rearrange("p two d -> p (two d)"), ident_bf[:])
+            nc.scalar.copy(out=rope_t[:], in_=bank[:])
+            bank = psum.tile([P, P], BF16, name="gain_turn", tag="turn", bufs=3)
+            nc.tensor.transpose(bank[:], head_rows[:], ident_bf[:])
+            nc.scalar.copy(out=gain_columns[:], in_=bank[:, :FUSED_HEADS])
+
+        def fill_diagonals(c):
+            for h in range(HEADS_PER_CHUNK):
+                head = (c - FIRST_FUSED_CHUNK) * HEADS_PER_CHUNK + h
+                nc.scalar.activation(out=diagonals[:, head, :], in_=ident_bf[:], func=ACT.Copy, scale=gain_columns[:, head:head + 1])
+
+        def fused_tables(p):
+            for which, banks, tag, bufs in ((1, gain_sin, "turn", 3), (0, gain_cos, "gain", 2)):
+                for c, t in units_of(p):
+                    first = (c - FIRST_FUSED_CHUNK) * HEADS_PER_CHUNK
+                    banks[c, t] = psum.tile([P, HEADS_PER_CHUNK, HD], F32, name="fused", tag=tag, bufs=bufs)
+                    nc.tensor.matmul(banks[c, t][:].rearrange("p h d -> p (h d)"), lhsT=rope_t[:, which, t, :],
+                                     rhs=diagonals[:, first:first + HEADS_PER_CHUNK, :].rearrange("p h d -> p (h d)"),
+                                     start=True, stop=True)
+
+        def fused_terms(p):
+            crossed[p] = ring.tile([P, 2, HEADS_PER_CHUNK, 2, HALF_HD], F32, name="crossed", tag="crossed", bufs=3)
+            for i, (c, t) in enumerate(units_of(p)):
+                factor = rstd[:, 1, t:t + 1] if p >= token_pairs else 1.0
+                z = result[:, t, c, :].rearrange("p (h d) -> p h d", d=HD)
+                for side in range(2):
+                    other = slice((1 - side) * HALF_HD, (2 - side) * HALF_HD)
+                    nc.vector.scalar_tensor_tensor(out=crossed[p][:, i, :, side, :], in0=z[:, :, other], scalar=factor,
+                                                   in1=gain_sin[c, t][:, :, other], op0=ALU.mult, op1=ALU.mult)
+            for c, t in units_of(p):
+                factor = rstd[:, 1, t:t + 1] if p >= token_pairs else 1.0
+                nc.vector.scalar_tensor_tensor(out=result[:, t, c, :], in0=result[:, t, c, :], scalar=factor,
+                                               in1=gain_cos[c, t][:].rearrange("p h d -> p (h d)"), op0=ALU.mult, op1=ALU.mult)
 
         def store(c, t):
             cols = slice((c % HALF_CHUNKS) * BANK, (c % HALF_CHUNKS + 1) * BANK)
@@ -266,21 +294,18 @@ def tile_dynamicselfattention_pa_kernel(tc, hidden_states, cos, sin, w_qk, b_qk,
         waiting = sorted((ready_step(p, t), t, c) for p in range(token_pairs) for c, t in units_of(p))
 
         spread_bias(0)
-        spread_gain(0)
-        spread_gain(1)
         for s in range(HEAD_PIECES):
-            reorder(s)
             turn(s)
             if s >= 2:
                 quantize(s - 2, 1)
         quantize(4, 1)
         multiply(0, 0)
-        reorder(6)
         quantize(5, 1)
         turn(6)
         multiply(0, 1)
+        spread_gain(0)
+        spread_gain(1)
         fill_tables()
-        reorder(7)
         turn(7)
         add_bias(0, 0)
         add_bias(0, 1)
@@ -305,12 +330,14 @@ def tile_dynamicselfattention_pa_kernel(tc, hidden_states, cos, sin, w_qk, b_qk,
         add_bias(0, 3)
         statistics(1)
 
+        nc.sync.dma_start(out=head_rows[0:FUSED_HEADS, :], in_=g_k[DIM - FUSED_HEADS * HD:].rearrange("(h d) -> h d", d=HD))
         done = 14
         unquantized = [12]
         for step in range(2, n_pairs + 3):
             runs = [] if done == len(pieces) else [done, done + 2] if step in DOUBLE_STEPS else [done]
             done += 2 * len(runs)
-            late = step - 2 if 5 <= step < n_pairs + 2 else None
+            late = step - 2 if 5 <= step < FIRST_FUSED_PAIR + 2 else None
+            fused = step - 2 if FIRST_FUSED_PAIR + 2 <= step < n_pairs + 2 else None
             if token_pairs <= step - 3:
                 for c, t in units_of(step - 3):
                     store(c, t)
@@ -319,15 +346,10 @@ def tile_dynamicselfattention_pa_kernel(tc, hidden_states, cos, sin, w_qk, b_qk,
                 join(1)
             if step == 4:
                 cos_term(2)
-            if late and unquantized:
+            if late:
                 apply_gain(late)
             if 3 <= step <= n_pairs:
                 add_bias(*units_of(step - 1)[0])
-            if late and not unquantized:
-                apply_gain(late)
-            if late:
-                cos_on_gpsimd(late)
-            if 3 <= step <= n_pairs:
                 add_bias(*units_of(step - 1)[1])
                 statistics(step - 1)
             if step in (2, 3):
@@ -336,7 +358,7 @@ def tile_dynamicselfattention_pa_kernel(tc, hidden_states, cos, sin, w_qk, b_qk,
             if group < CHUNKS // 2:
                 if step % 4 == 1:
                     spread_bias(group)
-                if step % 4 >= 2:
+                if step % 4 >= 2 and 2 * group + step % 2 < FIRST_FUSED_CHUNK:
                     spread_gain(2 * group + step % 2)
             if step < n_pairs:
                 for i in range(2):
@@ -344,10 +366,18 @@ def tile_dynamicselfattention_pa_kernel(tc, hidden_states, cos, sin, w_qk, b_qk,
                     for s in range(done - (2 - i) * len(runs), done - (1 - i) * len(runs)):
                         turn(s)
             if step == 2:
+                prepare_fused()
+            if 5 <= step < 5 + CHUNKS - FIRST_FUSED_CHUNK:
+                fill_diagonals(FIRST_FUSED_CHUNK + step - 5)
+            if fused:
+                fused_terms(fused)
+            if FIRST_FUSED_PAIR <= step - 1 < n_pairs:
+                fused_tables(step - 1)
+            if step == 2:
                 cos_term(1)
             if late:
                 cos_term(late)
-            if 4 <= step < n_pairs + 2:
+            if step == 4 or late:
                 sin_term(step - 2)
             for first in unquantized:
                 quantize(first, 2)

@@ -56,6 +56,7 @@ def tile_dynamicselfattention_pa_kernel(tc, hidden_states, cos, sin, w_qk, b_qk,
 
         raw = {}
         consumed = set()
+        ordered = {}
         gain_cos = {}
         gain_sin = {}
         grouped = {}
@@ -84,7 +85,9 @@ def tile_dynamicselfattention_pa_kernel(tc, hidden_states, cos, sin, w_qk, b_qk,
         load(0)
         nc.sync.dma_start(out=rows[0:CHUNKS, :], in_=b_qk.rearrange("(c n) -> c n", n=BANK))
         nc.sync.dma_start(out=rows[CHUNKS:CHUNKS + HALF_CHUNKS, :], in_=g_q.rearrange("(c n) -> c n", n=BANK))
-        nc.sync.dma_start(out=rows[CHUNKS + HALF_CHUNKS:2 * CHUNKS, :], in_=g_k.rearrange("(c n) -> c n", n=BANK))
+        plain_k = FIRST_FUSED_CHUNK - HALF_CHUNKS
+        nc.sync.dma_start(out=rows[CHUNKS + HALF_CHUNKS:CHUNKS + FIRST_FUSED_CHUNK, :],
+                          in_=g_k[:plain_k * BANK].rearrange("(c n) -> c n", n=BANK))
         for s in range(1, PASSES + 1):
             load(s)
 
@@ -122,6 +125,12 @@ def tile_dynamicselfattention_pa_kernel(tc, hidden_states, cos, sin, w_qk, b_qk,
             while len(raw) < len(pieces) and len(raw) - RAW_BUFS in consumed:
                 load(len(raw))
 
+        def reorder(s):
+            words = raw[s][:].rearrange("p j k -> p (j k)").bitcast(F32)
+            ordered[s] = ring.tile([P, 4, 2, P], F32, name="ordered", tag="ordered", bufs=2)
+            nc.vector.tensor_copy(out=ordered[s][:], in_=words.rearrange("p (j w u) -> p j u w", j=4, u=2))
+            release(s)
+
         def turn(s):
             if s < HEAD_PIECES or s % 2 == 0:
                 grouped[s] = ring.tile([P, 2, 4 * BANK], BF16, name="grouped", tag="grouped", bufs=4, align_bytes=64)
@@ -135,7 +144,8 @@ def tile_dynamicselfattention_pa_kernel(tc, hidden_states, cos, sin, w_qk, b_qk,
                 for jj in range(2):
                     for u in range(2):
                         j = 2 * b + jj
-                        nc.tensor.transpose(bank[:, jj, u, :], words[:, j, u:2 * P:2], ident[:])
+                        src = ordered[s][:, j, u, :] if s in ordered else words[:, j, u:2 * P:2]
+                        nc.tensor.transpose(bank[:, jj, u, :], src, ident[:])
                 nc.scalar.copy(out=dst[:, 2 * b:2 * b + 2], in_=bank[:].rearrange("p j u r -> p j r u"))
             release(s)
 
@@ -153,6 +163,9 @@ def tile_dynamicselfattention_pa_kernel(tc, hidden_states, cos, sin, w_qk, b_qk,
             nc.vector.quantize_mx(out=codes.rearrange("p a n -> p (a n)").bitcast(FP8X4),
                                   scales=scales.rearrange("p a n -> p (a n)"),
                                   in_=grouped[s][:, 0:count, :].rearrange("p a n -> p (a n)"))
+
+        def swap_sin():
+            nc.scalar.copy(out=sin_swapped[:], in_=sin_sb[:].rearrange("p t (two d) -> p t two d", two=2)[:, :, ::-1, :])
 
         def spread(dst, row):
             nc.tensor.matmul(dst, lhsT=ident_bf[:, row:row + 1].to_broadcast([P, P]), rhs=rows[:], start=True, stop=True)
@@ -231,7 +244,6 @@ def tile_dynamicselfattention_pa_kernel(tc, hidden_states, cos, sin, w_qk, b_qk,
                                     in1=signed_sin.to_broadcast([P, 2, HEADS_PER_CHUNK, 2, HALF_HD]), op=ALU.mult)
 
         def prepare_fused():
-            nc.scalar.copy(out=sin_swapped[:], in_=sin_sb[:].rearrange("p t (two d) -> p t two d", two=2)[:, :, ::-1, :])
             bank = psum.tile([P, 2, TOKEN_TILES, P], BF16, name="rope_turn", tag="turn", bufs=3)
             for t in range(TOKEN_TILES):
                 nc.tensor.transpose(bank[:, 0, t, :], cos_sb[:, t, :], ident_bf[:])
@@ -295,7 +307,13 @@ def tile_dynamicselfattention_pa_kernel(tc, hidden_states, cos, sin, w_qk, b_qk,
 
         spread_bias(0)
         for s in range(HEAD_PIECES):
+            reorder(s)
             turn(s)
+            if s in (0, 2):
+                spread_gain(s)
+                spread_gain(s + 1)
+            if s == 4:
+                spread_bias(1)
             if s >= 2:
                 quantize(s - 2, 1)
         quantize(4, 1)
@@ -303,8 +321,6 @@ def tile_dynamicselfattention_pa_kernel(tc, hidden_states, cos, sin, w_qk, b_qk,
         quantize(5, 1)
         turn(6)
         multiply(0, 1)
-        spread_gain(0)
-        spread_gain(1)
         fill_tables()
         turn(7)
         add_bias(0, 0)
@@ -313,19 +329,19 @@ def tile_dynamicselfattention_pa_kernel(tc, hidden_states, cos, sin, w_qk, b_qk,
         turn(8)
         turn(9)
         statistics(0)
+        swap_sin()
         multiply(0, 2)
+        apply_gain(0)
+        quantize(8, 2)
         turn(10)
         turn(11)
         multiply(0, 3)
         turn(12)
         turn(13)
-        spread_bias(1)
-        apply_gain(0)
-        quantize(8, 2)
         cos_term(0)
         add_bias(0, 2)
-        sin_term(0)
         quantize(10, 2)
+        sin_term(0)
         join(0)
         add_bias(0, 3)
         statistics(1)
@@ -352,13 +368,15 @@ def tile_dynamicselfattention_pa_kernel(tc, hidden_states, cos, sin, w_qk, b_qk,
                 add_bias(*units_of(step - 1)[0])
                 add_bias(*units_of(step - 1)[1])
                 statistics(step - 1)
+            if 5 <= step < 5 + CHUNKS - FIRST_FUSED_CHUNK:
+                fill_diagonals(FIRST_FUSED_CHUNK + step - 5)
             if step in (2, 3):
                 apply_gain(step - 1)
             group = step // 4 + 1
             if group < CHUNKS // 2:
                 if step % 4 == 1:
                     spread_bias(group)
-                if step % 4 >= 2 and 2 * group + step % 2 < FIRST_FUSED_CHUNK:
+                if step % 4 >= 2 and group >= 2 and 2 * group + step % 2 < FIRST_FUSED_CHUNK:
                     spread_gain(2 * group + step % 2)
             if step < n_pairs:
                 for i in range(2):
@@ -367,8 +385,6 @@ def tile_dynamicselfattention_pa_kernel(tc, hidden_states, cos, sin, w_qk, b_qk,
                         turn(s)
             if step == 2:
                 prepare_fused()
-            if 5 <= step < 5 + CHUNKS - FIRST_FUSED_CHUNK:
-                fill_diagonals(FIRST_FUSED_CHUNK + step - 5)
             if fused:
                 fused_terms(fused)
             if FIRST_FUSED_PAIR <= step - 1 < n_pairs:
@@ -377,10 +393,10 @@ def tile_dynamicselfattention_pa_kernel(tc, hidden_states, cos, sin, w_qk, b_qk,
                 cos_term(1)
             if late:
                 cos_term(late)
-            if step == 4 or late:
-                sin_term(step - 2)
             for first in unquantized:
                 quantize(first, 2)
+            if step == 4 or late:
+                sin_term(step - 2)
             unquantized = runs
             if 4 <= step < n_pairs + 2:
                 join(step - 2)

from contextlib import ExitStack

import concourse.mybir as mybir
from concourse.masks import make_identity

S, DIM, HD = 512, 2048, 128
EPS = 1e-6
FLOPS = 2 * S * DIM * 2 * DIM

F32 = mybir.dt.float32
BF16 = mybir.dt.bfloat16
U32 = mybir.dt.uint32
U8 = mybir.dt.uint8
FP8X4 = mybir.dt.float8_e5m2_x4
ALU = mybir.AluOpType
ACT = mybir.ActivationFunctionType

P = 128
BANK = 512
PASSES = DIM // BANK
TOKEN_TILES = S // P
CHUNKS = 2 * DIM // BANK
HALF_CHUNKS = CHUNKS // 2
HEADS_PER_CHUNK = BANK // HD
HALF_HD = HD // 2
RAW_BUFS = 10
HEAD_PIECES = PASSES + 2
FIRST_FUSED_PAIR = 10
FIRST_FUSED_CHUNK = FIRST_FUSED_PAIR // 2
FUSED_HEADS = (CHUNKS - FIRST_FUSED_CHUNK) * HEADS_PER_CHUNK
DOUBLE_STEPS = (4, 8)
NORMALISED_PER_STEP = 3


def tile_dynamicselfattention_pa_kernel(tc, hidden_states, cos, sin, w_qk, b_qk, g_q, g_k, out_0, out_1):
    nc = tc.nc
    x = hidden_states.rearrange("b (p t) k -> (b t) p k", t=TOKEN_TILES)
    outs = [o.rearrange("b (p t) h d -> (b t) p (h d)", t=TOKEN_TILES) for o in (out_0, out_1)]

    pieces = [("x", 0)] + [("w", 0, g) for g in range(PASSES)] + [("x", t) for t in range(1, TOKEN_TILES)]
    pieces += [("w", c, g) for c in range(1, CHUNKS) for g in range(PASSES)]
    n_pairs = CHUNKS * TOKEN_TILES // 2

    token_pairs = (CHUNKS - 2) * TOKEN_TILES // 2

    def units_of(p):
        if p < token_pairs:
            return [(p // 2, 2 * (p % 2) + i) for i in range(2)]
        return [(CHUNKS - 2 + i, p - token_pairs) for i in range(2)]

    with ExitStack() as ctx:
        keep = ctx.enter_context(tc.tile_pool(name="keep", bufs=1))
        ring = ctx.enter_context(tc.tile_pool(name="ring", bufs=3))
        psum = ctx.enter_context(tc.psum_pool(name="psum", bufs=2))
        ctx.enter_context(tc.manual_schedule())

        raw = {}
        consumed = set()
        ordered = {}
        gain_cos = {}
        gain_sin = {}
        grouped = {}
        w_codes = {}
        w_scales = {}
        acc = {}
        gained = {}
        crossed = {}
        gain_bank = {}
        bias = {}

        def load(s):
            piece = pieces[s]
            tile = ring.tile([P, 4, BANK], BF16, name="raw", tag="raw", bufs=RAW_BUFS)
            if piece[0] == "x":
                t = piece[1]
                src = x[t].rearrange("p (g k) -> p g k", g=PASSES)
            else:
                c, g = piece[1], piece[2]
                src = w_qk[c * BANK:(c + 1) * BANK, g * BANK:(g + 1) * BANK].rearrange("(j p) k -> p j k", p=P)
            nc.sync.dma_start(out=tile[:], in_=src)
            raw[s] = tile

        rows = keep.tile([P, BANK], BF16, name="rows")
        nc.vector.memset(rows[:], 0.0)
        load(0)
        nc.sync.dma_start(out=rows[0:CHUNKS, :], in_=b_qk.rearrange("(c n) -> c n", n=BANK))
        nc.sync.dma_start(out=rows[CHUNKS:CHUNKS + HALF_CHUNKS, :], in_=g_q.rearrange("(c n) -> c n", n=BANK))
        plain_k = FIRST_FUSED_CHUNK - HALF_CHUNKS
        nc.sync.dma_start(out=rows[CHUNKS + HALF_CHUNKS:CHUNKS + FIRST_FUSED_CHUNK, :],
                          in_=g_k[:plain_k * BANK].rearrange("(c n) -> c n", n=BANK))
        for s in range(1, PASSES + 1):
            load(s)

        ident = keep.tile([P, P], F32, name="ident")
        make_identity(nc, ident[:])
        ident_bf = keep.tile([P, P], BF16, name="ident_bf")
        make_identity(nc, ident_bf[:])
        minus_half = keep.tile([P, 2], F32, name="minus_half")
        nc.gpsimd.memset(minus_half[:], -0.5)

        load(PASSES + 1)
        cos_sb = keep.tile([P, TOKEN_TILES, HD], BF16, name="cos_sb")
        sin_sb = keep.tile([P, TOKEN_TILES, HD], BF16, name="sin_sb")
        nc.sync.dma_start(out=cos_sb[:], in_=cos.rearrange("(p t) d -> p t d", p=P))
        nc.sync.dma_start(out=sin_sb[:], in_=sin.rearrange("(p t) d -> p t d", p=P))
        for s in range(PASSES + 2, RAW_BUFS):
            load(s)

        head_rows = keep.tile([P, HD], BF16, name="head_rows")
        nc.gpsimd.memset(head_rows[:], 0.0)
        sin_swapped = keep.tile([P, TOKEN_TILES, 2, HALF_HD], BF16, name="sin_swapped")
        rope_t = keep.tile([P, 2, TOKEN_TILES, P], BF16, name="rope_t")
        gain_columns = keep.tile([P, FUSED_HEADS], F32, name="gain_columns")
        diagonals = keep.tile([P, FUSED_HEADS, HD], BF16, name="diagonals")
        x_codes = keep.tile([P, TOKEN_TILES, BANK], U32, name="x_codes", align_bytes=64)
        x_scales = keep.tile([P, TOKEN_TILES, BANK], U8, name="x_scales", align_bytes=64)
        result = keep.tile([P, TOKEN_TILES, CHUNKS, BANK], F32, name="result")
        partial = keep.tile([P, 2, TOKEN_TILES, HALF_CHUNKS], F32, name="partial")
        mean_eps = keep.tile([P, 2, TOKEN_TILES], F32, name="mean_eps")
        rstd = keep.tile([P, 2, TOKEN_TILES], F32, name="rstd")
        tables = psum.tile([P, 2, TOKEN_TILES, HD], BF16, name="tables", tag="tables", bufs=1)

        def release(s):
            consumed.add(s)
            while len(raw) < len(pieces) and len(raw) - RAW_BUFS in consumed:
                load(len(raw))

        def reorder(s):
            words = raw[s][:].rearrange("p j k -> p (j k)").bitcast(F32)
            ordered[s] = ring.tile([P, 4, 2, P], F32, name="ordered", tag="ordered", bufs=2)
            nc.vector.tensor_copy(out=ordered[s][:], in_=words.rearrange("p (j w u) -> p j u w", j=4, u=2))
            release(s)

        def turn(s):
            if s < HEAD_PIECES or s % 2 == 0:
                grouped[s] = ring.tile([P, 2, 4 * BANK], BF16, name="grouped", tag="grouped", bufs=4, align_bytes=64)
                tile, slot = grouped[s], 0
            else:
                tile, slot = grouped[s - 1], 1
            dst = tile[:, slot, :].bitcast(F32).rearrange("p (j r u) -> p j r u", j=4, u=2)
            words = raw[s][:].rearrange("p j k -> p (j k)").bitcast(F32).rearrange("p (j w) -> p j w", j=4)
            for b in range(2):
                bank = psum.tile([P, 2, 2, P], F32, name="turn", tag="turn", bufs=3)
                for jj in range(2):
                    for u in range(2):
                        j = 2 * b + jj
                        src = ordered[s][:, j, u, :] if s in ordered else words[:, j, u:2 * P:2]
                        nc.tensor.transpose(bank[:, jj, u, :], src, ident[:])
                nc.scalar.copy(out=dst[:, 2 * b:2 * b + 2], in_=bank[:].rearrange("p j u r -> p j r u"))
            release(s)

        def quantize(s, count):
            piece = pieces[s]
            if piece[0] == "x":
                t = piece[1]
                codes, scales = x_codes[:, t:t + count, :], x_scales[:, t:t + count, :]
            else:
                c, g = piece[1], piece[2]
                if g == 0:
                    w_codes[c] = ring.tile([P, PASSES, BANK], U32, name="w_codes", tag="w_codes", bufs=3, align_bytes=64)
                    w_scales[c] = ring.tile([P, PASSES, BANK], U8, name="w_scales", tag="w_scales", bufs=3, align_bytes=64)
                codes, scales = w_codes[c][:, g:g + count, :], w_scales[c][:, g:g + count, :]
            nc.vector.quantize_mx(out=codes.rearrange("p a n -> p (a n)").bitcast(FP8X4),
                                  scales=scales.rearrange("p a n -> p (a n)"),
                                  in_=grouped[s][:, 0:count, :].rearrange("p a n -> p (a n)"))

        def swap_sin():
            nc.scalar.copy(out=sin_swapped[:], in_=sin_sb[:].rearrange("p t (two d) -> p t two d", two=2)[:, :, ::-1, :])

        def spread(dst, row):
            nc.tensor.matmul(dst, lhsT=ident_bf[:, row:row + 1].to_broadcast([P, P]), rhs=rows[:], start=True, stop=True)

        def spread_bias(group):
            bank = psum.tile([P, 2, BANK], BF16, name="bias_bank", tag="turn", bufs=3)
            for i in range(2):
                spread(bank[:, i, :], 2 * group + i)
            bias[group] = ring.tile([P, 2, BANK], BF16, name="bias", tag="bias", bufs=2)
            nc.scalar.copy(out=bias[group][:], in_=bank[:])

        def spread_gain(c):
            if c % 2 == 0:
                gain_bank[c // 2] = psum.tile([P, 2, BANK], BF16, name="gain_bank", tag="gain", bufs=2)
            spread(gain_bank[c // 2][:, c % 2, :], CHUNKS + c)

        def fill_tables():
            nc.scalar.activation(out=sin_sb[:, :, :HALF_HD], in_=sin_sb[:, :, :HALF_HD], func=ACT.Copy, scale=-1.0)
            for i, src in enumerate((cos_sb, sin_sb)):
                nc.tensor.matmul(tables[:, i].rearrange("p t d -> p (t d)"), lhsT=ident_bf[:],
                                 rhs=src[:].rearrange("p t d -> p (t d)"), start=True, stop=True)

        def multiply(c, t):
            acc[c, t] = psum.tile([P, BANK], F32, name="acc", tag="acc", bufs=2)
            for g in range(PASSES):
                cols = slice(g * P, (g + 1) * P)
                nc.tensor.matmul_mx(
                    out=acc[c, t][:],
                    lhsT=x_codes[:, t, cols].bitcast(FP8X4), lhsT_scale=x_scales[:, t, cols],
                    rhs=w_codes[c][:, g, :].bitcast(FP8X4), rhs_scale=w_scales[c][:, g, :],
                    start=(g == 0), stop=(g == PASSES - 1))

        def pair_view(p):
            (c, t), (c_next, t_next) = units_of(p)
            return result[:, t:t_next + 1, c:c_next + 1, :].rearrange("p t c n -> p (t c) n")

        def pair_table(p, table):
            (c, t), (c_next, t_next) = units_of(p)
            return table[:, t:t_next + 1, :].to_broadcast([P, 2, HD])

        def add_bias(c, t):
            nc.vector.tensor_tensor(out=result[:, t, c, :], in0=acc[c, t][:], in1=bias[c // 2][:, c % 2, :], op=ALU.add)

        def statistics(p):
            for c, t in units_of(p):
                squares = ring.tile([P, BANK], F32, name="squares", tag="squares", bufs=2)
                nc.scalar.activation(out=squares[:], in_=result[:, t, c, :], func=ACT.Square,
                                     accum_out=partial[:, c // HALF_CHUNKS, t, c % HALF_CHUNKS:c % HALF_CHUNKS + 1])
            closed = [t for c, t in units_of(p) if c % HALF_CHUNKS == HALF_CHUNKS - 1]
            if closed:
                half = units_of(p)[0][0] // HALF_CHUNKS
                for t in closed:
                    shares = ring.tile([P, HALF_CHUNKS], F32, name="shares", tag="shares", bufs=2)
                    nc.scalar.activation(out=shares[:], in_=partial[:, half, t, :], func=ACT.Identity,
                                         scale=1.0 / DIM, bias=EPS / HALF_CHUNKS, accum_out=mean_eps[:, half, t:t + 1])
                span = slice(closed[0], closed[-1] + 1)
                nc.gpsimd.tensor_tensor(out=rstd[:, half, span], in0=mean_eps[:, half, span],
                                        in1=minus_half[:, :len(closed)], op=ALU.pow)

        def apply_gain(p):
            c = units_of(p)[0][0]
            gained[p] = ring.tile([P, 2, HEADS_PER_CHUNK, HD], F32, name="gained", tag="gained", bufs=3)
            dst = gained[p][:].rearrange("p t h d -> p t (h d)")
            gain = gain_bank[c // 2][:, c % 2:c % 2 + 1, :].to_broadcast([P, 2, BANK])
            nc.vector.tensor_tensor(out=dst, in0=pair_view(p), in1=gain, op=ALU.mult)

        def cos_term(p):
            table = pair_table(p, tables[:, 0]).unsqueeze(2).to_broadcast([P, 2, HEADS_PER_CHUNK, HD])
            nc.vector.tensor_tensor(out=pair_view(p).rearrange("p a (h d) -> p a h d", d=HD), in0=gained[p][:], in1=table, op=ALU.mult)

        def sin_term(p):
            crossed[p] = ring.tile([P, 2, HEADS_PER_CHUNK, 2, HALF_HD], F32, name="crossed", tag="crossed", bufs=3)
            swapped = gained[p][:].rearrange("p a h (two d) -> p a h two d", two=2)[:, :, :, ::-1, :]
            signed_sin = pair_table(p, tables[:, 1]).rearrange("p a (two d) -> p a two d", two=2).unsqueeze(2)
            nc.vector.tensor_tensor(out=crossed[p][:], in0=swapped,
                                    in1=signed_sin.to_broadcast([P, 2, HEADS_PER_CHUNK, 2, HALF_HD]), op=ALU.mult)

        def prepare_fused():
            bank = psum.tile([P, 2, TOKEN_TILES, P], BF16, name="rope_turn", tag="turn", bufs=3)
            for t in range(TOKEN_TILES):
                nc.tensor.transpose(bank[:, 0, t, :], cos_sb[:, t, :], ident_bf[:])
                nc.tensor.transpose(bank[:, 1, t, :], sin_swapped[:, t].rearrange("p two d -> p (two d)"), ident_bf[:])
            nc.scalar.copy(out=rope_t[:], in_=bank[:])
            bank = psum.tile([P, P], BF16, name="gain_turn", tag="turn", bufs=3)
            nc.tensor.transpose(bank[:], head_rows[:], ident_bf[:])
            nc.scalar.copy(out=gain_columns[:], in_=bank[:, :FUSED_HEADS])

        def fill_diagonals(c):
            for h in range(HEADS_PER_CHUNK):
                head = (c - FIRST_FUSED_CHUNK) * HEADS_PER_CHUNK + h
                nc.scalar.activation(out=diagonals[:, head, :], in_=ident_bf[:], func=ACT.Copy, scale=gain_columns[:, head:head + 1])

        def fused_tables(p):
            for which, banks, tag, bufs in ((1, gain_sin, "turn", 3), (0, gain_cos, "gain", 2)):
                for c, t in units_of(p):
                    first = (c - FIRST_FUSED_CHUNK) * HEADS_PER_CHUNK
                    banks[c, t] = psum.tile([P, HEADS_PER_CHUNK, HD], F32, name="fused", tag=tag, bufs=bufs)
                    nc.tensor.matmul(banks[c, t][:].rearrange("p h d -> p (h d)"), lhsT=rope_t[:, which, t, :],
                                     rhs=diagonals[:, first:first + HEADS_PER_CHUNK, :].rearrange("p h d -> p (h d)"),
                                     start=True, stop=True)

        def fused_terms(p):
            crossed[p] = ring.tile([P, 2, HEADS_PER_CHUNK, 2, HALF_HD], F32, name="crossed", tag="crossed", bufs=3)
            for i, (c, t) in enumerate(units_of(p)):
                factor = rstd[:, 1, t:t + 1] if p >= token_pairs else 1.0
                z = result[:, t, c, :].rearrange("p (h d) -> p h d", d=HD)
                for side in range(2):
                    other = slice((1 - side) * HALF_HD, (2 - side) * HALF_HD)
                    nc.vector.scalar_tensor_tensor(out=crossed[p][:, i, :, side, :], in0=z[:, :, other], scalar=factor,
                                                   in1=gain_sin[c, t][:, :, other], op0=ALU.mult, op1=ALU.mult)
            for c, t in units_of(p):
                factor = rstd[:, 1, t:t + 1] if p >= token_pairs else 1.0
                nc.vector.scalar_tensor_tensor(out=result[:, t, c, :], in0=result[:, t, c, :], scalar=factor,
                                               in1=gain_cos[c, t][:].rearrange("p h d -> p (h d)"), op0=ALU.mult, op1=ALU.mult)

        def store(c, t):
            cols = slice((c % HALF_CHUNKS) * BANK, (c % HALF_CHUNKS + 1) * BANK)
            nc.sync.dma_start(out=outs[c // HALF_CHUNKS][t][:, cols], in_=result[:, t, c, :])

        def join(p):
            cross = crossed[p][:].rearrange("p a h two d -> p a (h two d)")
            if p == n_pairs - 1:
                for i in range(2):
                    nc.vector.tensor_tensor(out=pair_view(p)[:, i, :], in0=pair_view(p)[:, i, :], in1=cross[:, i, :], op=ALU.add)
            else:
                nc.gpsimd.tensor_tensor(out=pair_view(p), in0=pair_view(p), in1=cross, op=ALU.add)

        def normalise(c, t):
            nc.scalar.activation(out=result[:, t, c, :], in_=result[:, t, c, :], func=ACT.Copy,
                                 scale=rstd[:, c // HALF_CHUNKS, t:t + 1])
            store(c, t)

        def ready_step(p, t):
            if p < n_pairs // 2:
                return max(p + 3, n_pairs // 2 + t // 2)
            return token_pairs + t + 1

        waiting = sorted((ready_step(p, t), t, c) for p in range(token_pairs) for c, t in units_of(p))

        spread_bias(0)
        for s in range(HEAD_PIECES):
            reorder(s)
            turn(s)
            if s in (0, 2):
                spread_gain(s)
                spread_gain(s + 1)
            if s == 4:
                spread_bias(1)
            if s >= 2:
                quantize(s - 2, 1)
        quantize(4, 1)
        multiply(0, 0)
        quantize(5, 1)
        turn(6)
        multiply(0, 1)
        fill_tables()
        turn(7)
        add_bias(0, 0)
        add_bias(0, 1)
        quantize(6, 2)
        turn(8)
        turn(9)
        statistics(0)
        swap_sin()
        multiply(0, 2)
        apply_gain(0)
        quantize(8, 2)
        turn(10)
        turn(11)
        multiply(0, 3)
        turn(12)
        turn(13)
        cos_term(0)
        add_bias(0, 2)
        quantize(10, 2)
        sin_term(0)
        join(0)
        add_bias(0, 3)
        statistics(1)

        nc.sync.dma_start(out=head_rows[0:FUSED_HEADS, :], in_=g_k[DIM - FUSED_HEADS * HD:].rearrange("(h d) -> h d", d=HD))
        done = 14
        unquantized = [12]
        for step in range(2, n_pairs + 3):
            runs = [] if done == len(pieces) else [done, done + 2] if step in DOUBLE_STEPS else [done]
            done += 2 * len(runs)
            late = step - 2 if 5 <= step < FIRST_FUSED_PAIR + 2 else None
            fused = step - 2 if FIRST_FUSED_PAIR + 2 <= step < n_pairs + 2 else None
            if token_pairs <= step - 3:
                for c, t in units_of(step - 3):
                    store(c, t)
            if step == 3:
                sin_term(1)
                join(1)
            if step == 4:
                cos_term(2)
            if late:
                apply_gain(late)
            if 3 <= step <= n_pairs:
                add_bias(*units_of(step - 1)[0])
                add_bias(*units_of(step - 1)[1])
                statistics(step - 1)
            if 5 <= step < 5 + CHUNKS - FIRST_FUSED_CHUNK:
                fill_diagonals(FIRST_FUSED_CHUNK + step - 5)
            if step in (2, 3):
                apply_gain(step - 1)
            group = step // 4 + 1
            if group < CHUNKS // 2:
                if step % 4 == 1:
                    spread_bias(group)
                if step % 4 >= 2 and group >= 2 and 2 * group + step % 2 < FIRST_FUSED_CHUNK:
                    spread_gain(2 * group + step % 2)
            if step < n_pairs:
                for i in range(2):
                    multiply(*units_of(step)[i])
                    for s in range(done - (2 - i) * len(runs), done - (1 - i) * len(runs)):
                        turn(s)
            if step == 2:
                prepare_fused()
            if fused:
                fused_terms(fused)
            if FIRST_FUSED_PAIR <= step - 1 < n_pairs:
                fused_tables(step - 1)
            if step == 2:
                cos_term(1)
            if late:
                cos_term(late)
            for first in unquantized:
                quantize(first, 2)
            if step == 4 or late:
                sin_term(step - 2)
            unquantized = runs
            if 4 <= step < n_pairs + 2:
                join(step - 2)
            for ready, t, c in waiting[:NORMALISED_PER_STEP]:
                if ready <= step:
                    waiting.remove((ready, t, c))
                    normalise(c, t)
        assert not waiting
